import numpy as np
import ml_dtypes


def mxq(x, axis, fmt="e4m3"):
    dtype, down = {"e4m3": (ml_dtypes.float8_e4m3fn, 7), "e5m2": (ml_dtypes.float8_e5m2, 14)}[fmt]
    v = np.moveaxis(np.asarray(x, np.float32).astype(ml_dtypes.bfloat16).astype(np.float64), axis, -1)
    blocks = v.reshape(v.shape[:-1] + (-1, 32))
    amax = np.abs(blocks).max(-1, keepdims=True)
    byte = np.maximum(np.where(amax > 0, np.frexp(amax)[1] - 1 + 127, 0) - down, 1)
    scale = np.exp2(byte - 127.0)
    codes = (blocks / scale).astype(np.float32).astype(dtype).astype(np.float64)
    return np.moveaxis((codes * scale).reshape(v.shape), -1, axis)


WIDE = False


def mx_kscale(k):
    if not WIDE:
        return np.ones(k)
    levels = np.array([10, -10, 5, -5, 0])
    if k % 512:
        return np.exp2(np.random.permutation(np.resize(levels, k // 32))).repeat(32)
    a = np.empty((k // 512, 16))
    for p in range(k // 512):
        a[p, :8] = np.random.permutation(np.resize(levels, 8))
        for g in range(8):
            far = levels[np.abs(levels - a[p, g]) >= 10]
            a[p, g + 8] = far[np.random.randint(len(far))]
    return np.exp2(a.ravel()).repeat(32)


BF16 = ml_dtypes.bfloat16


def bf(x):
    return np.asarray(x, np.float32).astype(BF16)


def f64(x):
    return np.asarray(x).astype(np.float64)


B, CH, C1, C2, D, NF, W, H = 1, 1024, 128, 512, 2, 8, 16, 16
N = NF * W * H
M = NF * (W // D) * (H // D)


def conv(xq, w, b):
    return (mxq(f64(w), 1, "e4m3") @ xq) + f64(b)[None, :, None]


def maxpool_wh(v):
    return v.reshape(B, -1, NF, W // D, D, H // D, D).max(axis=(4, 6)).reshape(B, -1, M)


def setup_inputs():
    s = mx_kscale(CH)
    return {"x": bf(np.random.standard_normal((B, CH, NF, W, H)) * s[None, :, None, None, None]),
            "w_theta": bf(np.random.standard_normal((C1, CH)) * 0.3 / np.sqrt(CH) / s),
            "b_theta": bf(np.random.standard_normal(C1) * 0.1),
            "w_phi": bf(np.random.standard_normal((C1, CH)) * 0.3 / np.sqrt(CH) / s),
            "b_phi": bf(np.random.standard_normal(C1) * 0.1),
            "w_g": bf(np.random.standard_normal((C2, CH)) / np.sqrt(CH) / s),
            "b_g": bf(np.random.standard_normal(C2) * 0.2)}


def reference(x, w_theta, b_theta, w_phi, b_phi, w_g, b_g):
    xq = mxq(f64(x).reshape(B, CH, N), 1, "e4m3")
    theta = np.tanh(conv(xq, w_theta, b_theta)).transpose(0, 2, 1)
    phi = maxpool_wh(np.tanh(conv(xq, w_phi, b_phi))).transpose(0, 2, 1)
    g = maxpool_wh(conv(xq, w_g, b_g)).transpose(0, 2, 1)
    return theta, phi, g

@@ -1,0 +1,309 @@
+from contextlib import ExitStack
+
+import concourse.mybir as mybir
+from concourse.masks import make_identity
+
+FLOPS = 2 * (128 + 128 + 512) * 1024 * 2048
+
+BF16 = mybir.dt.bfloat16
+F32 = mybir.dt.float32
+U32 = mybir.dt.uint32
+U8 = mybir.dt.uint8
+FP8X4 = mybir.dt.float8_e4m3fn_x4
+ALU = mybir.AluOpType
+ACT = mybir.ActivationFunctionType
+
+P = 128
+PACK = 4
+PASSES = 2
+HALVES = 2
+CHANNELS = 1024
+CHUNKS = 4
+CHUNK = 512
+WINDOW_ROWS = 16
+WINDOW_COLS = 8
+MEMBERS = 4
+C_G = 512
+C_PHI = 128
+C_THETA = 128
+BLOCK = 256
+BANK = 512
+PSUM_BANKS = 8
+
+
+def tile_selfattention3d_pb_kernel(
+    tc, x, w_theta, b_theta, w_phi, b_phi, w_g, b_g, out_0, out_1, out_2
+):
+    nc = tc.nc
+
+    x_pieces = x.rearrange("o (c p k) f i j -> (o c) p k (f i j)", c=PASSES, p=P, k=PACK)
+    theta_rows = out_0.rearrange("o (t j p) c -> (o t) p j c", t=CHUNKS, p=P)
+    phi_rows = out_1.rearrange("o (t w) c -> (o t) w c", t=CHUNKS)
+    g_rows = out_2.rearrange("o (t w) c -> (o t) w c", t=CHUNKS)
+    w_g_tiles = w_g.rearrange("(r p) k -> p r k", p=P)
+
+    with ExitStack() as ctx:
+        consts = ctx.enter_context(tc.tile_pool(name="consts", bufs=1))
+        per_chunk = ctx.enter_context(tc.tile_pool(name="per_chunk", bufs=CHUNKS))
+        results = ctx.enter_context(tc.tile_pool(name="results", bufs=CHUNKS))
+        psum = ctx.enter_context(tc.psum_pool(name="psum", bufs=PSUM_BANKS))
+
+        raws = [per_chunk.tile([P, PASSES, PACK, CHUNK], BF16, name="raw") for t in range(CHUNKS)]
+        groupeds = [
+            per_chunk.tile([P, PASSES, MEMBERS, P, PACK], BF16, align_bytes=64, name="grouped")
+            for t in range(CHUNKS)
+        ]
+        x_codes = [
+            per_chunk.tile([P, PASSES, MEMBERS, P], U32, align_bytes=64, name="x_codes")
+            for t in range(CHUNKS)
+        ]
+        x_scales = [
+            per_chunk.tile([P, PASSES, MEMBERS, P], U8, align_bytes=64, name="x_scales")
+            for t in range(CHUNKS)
+        ]
+
+        def load_chunk(t):
+            for c in range(PASSES):
+                nc.sync.dma_start(
+                    out=raws[t][:, c, :, :],
+                    in_=x_pieces[c, :, :, t * CHUNK : (t + 1) * CHUNK],
+                )
+
+        w_rows = consts.tile([P, 6, CHANNELS], BF16)
+        load_chunk(0)
+        nc.sync.dma_start(out=w_rows[:, 4, :], in_=w_phi)
+        nc.sync.dma_start(out=w_rows[:, 5, :], in_=w_theta)
+        nc.sync.dma_start(out=w_rows[:, 0:2, :], in_=w_g_tiles[:, 0:2, :])
+        nc.sync.dma_start(out=w_rows[:, 2:4, :], in_=w_g_tiles[:, 2:4, :])
+        for t in range(1, CHUNKS):
+            load_chunk(t)
+
+        warm = consts.tile([P, 1], F32)
+        nc.vector.memset(warm[:], 0.0)
+        nc.scalar.activation(out=warm[:], in_=warm[:], func=ACT.Tanh)
+
+        ident = consts.tile([P, P], F32)
+        make_identity(nc, ident[:])
+
+        bias_rows = consts.tile([P, C_G + C_PHI + C_THETA], BF16)
+        nc.vector.memset(bias_rows[:], 0.0)
+        nc.scalar.dma_start(out=bias_rows[0:1, 0:C_G], in_=b_g.rearrange("(o n) -> o n", o=1))
+        nc.scalar.dma_start(
+            out=bias_rows[0:1, C_G : C_G + C_PHI], in_=b_phi.rearrange("(o n) -> o n", o=1)
+        )
+        nc.scalar.dma_start(
+            out=bias_rows[0:1, C_G + C_PHI :], in_=b_theta.rearrange("(o n) -> o n", o=1)
+        )
+        ones = consts.tile([P, P], BF16)
+        nc.vector.memset(ones[:], 1.0)
+        bias = consts.tile([P, C_G + C_PHI], F32)
+        for first, width in ((0, C_G), (C_G, C_PHI)):
+            bias_bank = psum.tile([P, BANK], F32, tag="bank")
+            nc.tensor.matmul(
+                out=bias_bank[:, 0:width],
+                lhsT=ones[:],
+                rhs=bias_rows[:, first : first + width],
+                start=True,
+                stop=True,
+            )
+            nc.scalar.copy(out=bias[:, first : first + width], in_=bias_bank[:, 0:width])
+        bias_theta_bank = psum.tile([P, BANK], F32, tag="bank")
+        nc.tensor.matmul(
+            out=bias_theta_bank[:, 0:P],
+            lhsT=bias_rows[:, C_G + C_PHI :],
+            rhs=ones[:],
+            start=True,
+            stop=True,
+        )
+        bias_theta = consts.tile([P, 1], F32)
+        nc.scalar.copy(out=bias_theta[:], in_=bias_theta_bank[:, 0:1])
+
+        def regroup(q):
+            t, c = divmod(q, PASSES)
+            if t >= CHUNKS:
+                return
+            by_member = raws[t][:, c, :, :].rearrange(
+                "p k (a di b dj) -> p di dj a b k", a=WINDOW_ROWS, di=2, b=WINDOW_COLS, dj=2
+            )
+            for di in range(2):
+                if di == 0:
+                    nc.vector.tensor_copy(
+                        out=groupeds[t][:, c, 0:2, :, :].rearrange(
+                            "p dj (a b) k -> p a b k dj", a=WINDOW_ROWS
+                        ),
+                        in_=raws[t][:, c, :, :].rearrange(
+                            "p k (a di b dj) -> p di a b k dj",
+                            a=WINDOW_ROWS, di=2, b=WINDOW_COLS, dj=2,
+                        )[:, 0],
+                    )
+                else:
+                    for dj in range(2):
+                        nc.scalar.copy(
+                            out=groupeds[t][:, c, 2 * di + dj, :, :].rearrange(
+                                "p (a b) k -> p a b k", a=WINDOW_ROWS
+                            ),
+                            in_=by_member[:, di, dj],
+                        )
+
+        def quantise(t, c):
+            if t >= CHUNKS:
+                return
+            nc.vector.quantize_mx(
+                out=x_codes[t][:, c, :, :].rearrange("p m w -> p (m w)").bitcast(FP8X4),
+                scales=x_scales[t][:, c, :, :].rearrange("p m w -> p (m w)"),
+                in_=groupeds[t][:, c, :, :, :].rearrange("p m w k -> p (m w k)"),
+            )
+
+        def prepare_weights(first_row_tile):
+            grouped = consts.tile(
+                [P, PASSES, BLOCK * PACK], BF16, align_bytes=64,
+                name="w_grouped%d" % first_row_tile,
+            )
+            for c in range(PASSES):
+                w_bank = psum.tile([P, 2, HALVES, P], F32, tag="bank")
+                for r in range(2):
+                    words = w_rows[:, first_row_tile + r, :].bitcast(F32)
+                    for u in range(HALVES):
+                        pass_words = slice(HALVES * P * c + u, HALVES * P * (c + 1), HALVES)
+                        nc.tensor.transpose(w_bank[:, r, u, :], words[:, pass_words], ident[:])
+                out_words = grouped[:, c, :].bitcast(F32).rearrange(
+                    "p (r o u) -> p r o u", r=2, u=HALVES
+                )
+                in_words = w_bank[:].rearrange("p r u o -> p r o u")
+                nc.scalar.copy(out=out_words, in_=in_words)
+            codes = consts.tile(
+                [P, PASSES, BLOCK], U32, align_bytes=64, name="w_codes%d" % first_row_tile
+            )
+            scales = consts.tile(
+                [P, PASSES, BLOCK], U8, align_bytes=64, name="w_scales%d" % first_row_tile
+            )
+            nc.vector.quantize_mx(
+                out=codes[:].rearrange("p c n -> p (c n)").bitcast(FP8X4),
+                scales=scales[:].rearrange("p c n -> p (c n)"),
+                in_=grouped[:].rearrange("p c n -> p (c n)"),
+            )
+            return codes, scales
+
+        def product(out, t, member, weights, first, width):
+            w_codes, w_scales = weights
+            for c in range(PASSES):
+                nc.tensor.matmul_mx(
+                    out=out,
+                    lhsT=x_codes[t][:, c, member, :].bitcast(FP8X4),
+                    lhsT_scale=x_scales[t][:, c, member, :],
+                    rhs=w_codes[:, c, first : first + width].bitcast(FP8X4),
+                    rhs_scale=w_scales[:, c, first : first + width],
+                    start=(c == 0),
+                    stop=(c == PASSES - 1),
+                )
+
+        theta_banks = {}
+        phi_banks = {}
+        g_banks = {}
+
+        def products(t):
+            if t >= CHUNKS:
+                return
+            w_codes, w_scales = w_small
+            theta_bank = psum.tile([P, MEMBERS * P], F32, tag="bank")
+            for c in range(PASSES):
+                nc.tensor.matmul_mx(
+                    out=theta_bank[:],
+                    lhsT=w_codes[:, c, C_PHI : C_PHI + C_THETA].bitcast(FP8X4),
+                    lhsT_scale=w_scales[:, c, C_PHI : C_PHI + C_THETA],
+                    rhs=x_codes[t][:, c, :, :].rearrange("p m w -> p (m w)").bitcast(FP8X4),
+                    rhs_scale=x_scales[t][:, c, :, :].rearrange("p m w -> p (m w)"),
+                    start=(c == 0),
+                    stop=(c == PASSES - 1),
+                )
+            theta_banks[t] = theta_bank
+            phi_bank = psum.tile([P, MEMBERS, C_PHI], F32, tag="bank")
+            for member in range(MEMBERS):
+                product(phi_bank[:, member, :], t, member, w_small, 0, C_PHI)
+            phi_banks[t] = phi_bank
+            for member in range(MEMBERS):
+                g_bank = psum.tile([P, C_G], F32, tag="bank")
+                product(g_bank[:, 0:BLOCK], t, member, w_g_low, 0, BLOCK)
+                product(g_bank[:, BLOCK:C_G], t, member, w_g_high, 0, BLOCK)
+                g_banks[t, member] = g_bank
+
+        pooleds = {}
+
+        def copy_first_member(t):
+            pooled = results.tile([P, C_G + C_PHI], F32, name="pooled")
+            nc.scalar.copy(out=pooled[:, 0:C_G], in_=g_banks[t, 0][:])
+            pooleds[t] = pooled
+
+        def tanh_theta_store(t):
+            by_channel = results.tile([P, CHUNK], F32, name="theta_by_channel")
+            for di in range(2):
+                nc.scalar.activation(
+                    out=by_channel[:].rearrange(
+                        "p (a di b dj) -> p di a b dj", a=WINDOW_ROWS, di=2, b=WINDOW_COLS, dj=2
+                    )[:, di],
+                    in_=theta_banks[t][:].rearrange(
+                        "p (di dj a b) -> p di a b dj", di=2, dj=2, a=WINDOW_ROWS, b=WINDOW_COLS
+                    )[:, di],
+                    func=ACT.Tanh,
+                    bias=bias_theta[:],
+                    scale=1.0,
+                )
+            flipped = psum.tile([P, CHUNK // P, C_THETA], F32, tag="bank")
+            for j in range(CHUNK // P):
+                nc.tensor.transpose(flipped[:, j, :], by_channel[:, j * P : (j + 1) * P], ident[:])
+            theta = results.tile([P, CHUNK // P, C_THETA], F32, name="theta")
+            nc.scalar.copy(out=theta[:], in_=flipped[:])
+            nc.sync.dma_start(out=theta_rows[t], in_=theta[:])
+
+        def pool_phi(t):
+            nc.vector.tensor_reduce(
+                out=pooleds[t][:, C_G:],
+                in_=phi_banks[t][:].rearrange("p m c -> p c m"),
+                axis=mybir.AxisListType.X,
+                op=ALU.max,
+            )
+
+        def max_g(t, member):
+            nc.vector.tensor_tensor(
+                out=pooleds[t][:, 0:C_G],
+                in0=g_banks[t, member][:],
+                in1=pooleds[t][:, 0:C_G],
+                op=ALU.max,
+            )
+
+        def add_pooled_bias_store(t):
+            pooled = pooleds[t]
+            adder = nc.vector if t == CHUNKS - 1 else nc.gpsimd
+            for columns in (slice(C_G, C_G + C_PHI), slice(0, C_G)):
+                adder.tensor_tensor(
+                    out=pooled[:, columns], in0=pooled[:, columns], in1=bias[:, columns], op=ALU.add
+                )
+            nc.sync.dma_start(out=g_rows[t], in_=pooled[:, 0:C_G])
+
+        def tanh_phi_store(t):
+            phi = results.tile([P, C_PHI], F32, name="phi")
+            nc.scalar.activation(out=phi[:], in_=pooleds[t][:, C_G:], func=ACT.Tanh)
+            nc.sync.dma_start(out=phi_rows[t], in_=phi[:])
+
+        regroup(0)
+        regroup(1)
+        quantise(0, 0)
+        quantise(0, 1)
+        w_small = prepare_weights(4)
+        w_g_low = prepare_weights(0)
+        w_g_high = prepare_weights(2)
+        products(0)
+        for t in range(CHUNKS):
+            regroup(PASSES * t + 2)
+            regroup(PASSES * t + 3)
+            quantise(t + 1, 0)
+            quantise(t + 1, 1)
+            products(t + 1)
+            copy_first_member(t)
+            tanh_theta_store(t)
+            pool_phi(t)
+            max_g(t, 1)
+            max_g(t, 2)
+            max_g(t, 3)
+            add_pooled_bias_store(t)
+            tanh_phi_store(t)

@@ -29,6 +29,9 @@ C_THETA = 128
 BLOCK = 256
 BANK = 512
 PSUM_BANKS = 8
+SMALL = 4
+G_LOW = 0
+G_HIGH = 2
 
 
 def tile_selfattention3d_pb_kernel(
@@ -62,103 +65,100 @@ def tile_selfattention3d_pb_kernel(
             for t in range(CHUNKS)
         ]
 
-        def load_chunk(t):
-            for c in range(PASSES):
-                nc.sync.dma_start(
-                    out=raws[t][:, c, :, :],
-                    in_=x_pieces[c, :, :, t * CHUNK : (t + 1) * CHUNK],
-                )
-
         w_rows = consts.tile([P, 6, CHANNELS], BF16)
-        load_chunk(0)
-        nc.sync.dma_start(out=w_rows[:, 4, :], in_=w_phi)
-        nc.sync.dma_start(out=w_rows[:, 5, :], in_=w_theta)
-        nc.sync.dma_start(out=w_rows[:, 0:2, :], in_=w_g_tiles[:, 0:2, :])
-        nc.sync.dma_start(out=w_rows[:, 2:4, :], in_=w_g_tiles[:, 2:4, :])
-        for t in range(1, CHUNKS):
-            load_chunk(t)
-
-        warm = consts.tile([P, 1], F32)
-        nc.vector.memset(warm[:], 0.0)
-        nc.scalar.activation(out=warm[:], in_=warm[:], func=ACT.Tanh)
-
-        ident = consts.tile([P, P], F32)
-        make_identity(nc, ident[:])
-
         bias_rows = consts.tile([P, C_G + C_PHI + C_THETA], BF16)
-        nc.vector.memset(bias_rows[:], 0.0)
-        nc.scalar.dma_start(out=bias_rows[0:1, 0:C_G], in_=b_g.rearrange("(o n) -> o n", o=1))
-        nc.scalar.dma_start(
-            out=bias_rows[0:1, C_G : C_G + C_PHI], in_=b_phi.rearrange("(o n) -> o n", o=1)
-        )
-        nc.scalar.dma_start(
-            out=bias_rows[0:1, C_G + C_PHI :], in_=b_theta.rearrange("(o n) -> o n", o=1)
-        )
-        ones = consts.tile([P, P], BF16)
-        nc.vector.memset(ones[:], 1.0)
         bias = consts.tile([P, C_G + C_PHI], F32)
-        for first, width in ((0, C_G), (C_G, C_PHI)):
-            bias_bank = psum.tile([P, BANK], F32, tag="bank")
+        bias_theta = consts.tile([P, 1], F32)
+        ones = consts.tile([P, P], BF16)
+        ident = consts.tile([P, P], F32)
+        warm = consts.tile([P, 1], F32)
+
+        def load_x(t, c):
+            nc.sync.dma_start(
+                out=raws[t][:, c, :, :], in_=x_pieces[c, :, :, t * CHUNK : (t + 1) * CHUNK]
+            )
+
+        def load_all():
+            load_x(0, 0)
+            for vec, first, width in (
+                (b_g, 0, C_G), (b_phi, C_G, C_PHI), (b_theta, C_G + C_PHI, C_THETA)
+            ):
+                nc.sync.dma_start(
+                    out=bias_rows[0:1, first : first + width],
+                    in_=vec.rearrange("(o n) -> o n", o=1),
+                )
+            nc.sync.dma_start(out=w_rows[:, 4, :], in_=w_phi)
+            nc.sync.dma_start(out=w_rows[:, 5, :], in_=w_theta)
+            load_x(0, 1)
+            nc.sync.dma_start(out=w_rows[:, 0:2, :], in_=w_g_tiles[:, 0:2, :])
+            nc.sync.dma_start(out=w_rows[:, 2:4, :], in_=w_g_tiles[:, 2:4, :])
+            for t in range(1, CHUNKS):
+                for c in range(PASSES):
+                    load_x(t, c)
+
+        def constants():
+            nc.vector.memset(warm[:], 0.0)
+            nc.vector.memset(ones[:], 1.0)
+            nc.scalar.activation(out=warm[:], in_=warm[:], func=ACT.Tanh)
+            make_identity(nc, ident[:])
+
+        def spread_biases():
+            for first, width in ((0, C_G), (C_G, C_PHI)):
+                bias_bank = psum.tile([P, BANK], F32, tag="bank")
+                nc.tensor.matmul(
+                    out=bias_bank[:, 0:width],
+                    lhsT=ones[:],
+                    rhs=bias_rows[:, first : first + width],
+                    start=True,
+                    stop=True,
+                )
+                nc.scalar.copy(out=bias[:, first : first + width], in_=bias_bank[:, 0:width])
+            bias_theta_bank = psum.tile([P, BANK], F32, tag="bank")
             nc.tensor.matmul(
-                out=bias_bank[:, 0:width],
-                lhsT=ones[:],
-                rhs=bias_rows[:, first : first + width],
+                out=bias_theta_bank[:, 0:P],
+                lhsT=bias_rows[:, C_G + C_PHI :],
+                rhs=ones[:],
                 start=True,
                 stop=True,
             )
-            nc.scalar.copy(out=bias[:, first : first + width], in_=bias_bank[:, 0:width])
-        bias_theta_bank = psum.tile([P, BANK], F32, tag="bank")
-        nc.tensor.matmul(
-            out=bias_theta_bank[:, 0:P],
-            lhsT=bias_rows[:, C_G + C_PHI :],
-            rhs=ones[:],
-            start=True,
-            stop=True,
-        )
-        bias_theta = consts.tile([P, 1], F32)
-        nc.scalar.copy(out=bias_theta[:], in_=bias_theta_bank[:, 0:1])
+            nc.scalar.copy(out=bias_theta[:], in_=bias_theta_bank[:, 0:1])
 
-        def regroup(q):
-            t, c = divmod(q, PASSES)
-            if t >= CHUNKS:
-                return
+        def regroup_vector(t, c):
+            nc.vector.tensor_copy(
+                out=groupeds[t][:, c, 0:2, :, :].rearrange(
+                    "p dj (a b) k -> p a b k dj", a=WINDOW_ROWS
+                ),
+                in_=raws[t][:, c, :, :].rearrange(
+                    "p k (a di b dj) -> p di a b k dj", a=WINDOW_ROWS, di=2, b=WINDOW_COLS, dj=2
+                )[:, 0],
+            )
+
+        def regroup_scalar(t, c):
             by_member = raws[t][:, c, :, :].rearrange(
                 "p k (a di b dj) -> p di dj a b k", a=WINDOW_ROWS, di=2, b=WINDOW_COLS, dj=2
             )
-            for di in range(2):
-                if di == 0:
-                    nc.vector.tensor_copy(
-                        out=groupeds[t][:, c, 0:2, :, :].rearrange(
-                            "p dj (a b) k -> p a b k dj", a=WINDOW_ROWS
-                        ),
-                        in_=raws[t][:, c, :, :].rearrange(
-                            "p k (a di b dj) -> p di a b k dj",
-                            a=WINDOW_ROWS, di=2, b=WINDOW_COLS, dj=2,
-                        )[:, 0],
-                    )
-                else:
-                    for dj in range(2):
-                        nc.scalar.copy(
-                            out=groupeds[t][:, c, 2 * di + dj, :, :].rearrange(
-                                "p (a b) k -> p a b k", a=WINDOW_ROWS
-                            ),
-                            in_=by_member[:, di, dj],
-                        )
+            for dj in range(2):
+                nc.scalar.copy(
+                    out=groupeds[t][:, c, 2 + dj, :, :].rearrange("p (a b) k -> p a b k", a=WINDOW_ROWS),
+                    in_=by_member[:, 1, dj],
+                )
+
+        def regroup(t, c):
+            regroup_vector(t, c)
+            regroup_scalar(t, c)
 
         def quantise(t, c):
-            if t >= CHUNKS:
-                return
             nc.vector.quantize_mx(
                 out=x_codes[t][:, c, :, :].rearrange("p m w -> p (m w)").bitcast(FP8X4),
                 scales=x_scales[t][:, c, :, :].rearrange("p m w -> p (m w)"),
                 in_=groupeds[t][:, c, :, :, :].rearrange("p m w k -> p (m w k)"),
             )
 
-        def prepare_weights(first_row_tile):
-            grouped = consts.tile(
-                [P, PASSES, BLOCK * PACK], BF16, align_bytes=64,
-                name="w_grouped%d" % first_row_tile,
-            )
+        w_grouped = {}
+        w_banks = {}
+        weights = {}
+
+        def transpose_weights(first_row_tile):
             for c in range(PASSES):
                 w_bank = psum.tile([P, 2, HALVES, P], F32, tag="bank")
                 for r in range(2):
@@ -166,11 +166,21 @@ def tile_selfattention3d_pb_kernel(
                     for u in range(HALVES):
                         pass_words = slice(HALVES * P * c + u, HALVES * P * (c + 1), HALVES)
                         nc.tensor.transpose(w_bank[:, r, u, :], words[:, pass_words], ident[:])
-                out_words = grouped[:, c, :].bitcast(F32).rearrange(
-                    "p (r o u) -> p r o u", r=2, u=HALVES
+                w_banks[first_row_tile, c] = w_bank
+
+        def copy_weights(first_row_tile):
+            grouped = consts.tile(
+                [P, PASSES, BLOCK * PACK], BF16, align_bytes=64,
+                name="w_grouped%d" % first_row_tile,
+            )
+            for c in range(PASSES):
+                nc.scalar.copy(
+                    out=grouped[:, c, :].bitcast(F32).rearrange("p (r o u) -> p r o u", r=2, u=HALVES),
+                    in_=w_banks[first_row_tile, c][:].rearrange("p r u o -> p r o u"),
                 )
-                in_words = w_bank[:].rearrange("p r u o -> p r o u")
-                nc.scalar.copy(out=out_words, in_=in_words)
+            w_grouped[first_row_tile] = grouped
+
+        def quantise_weights(first_row_tile):
             codes = consts.tile(
                 [P, PASSES, BLOCK], U32, align_bytes=64, name="w_codes%d" % first_row_tile
             )
@@ -180,12 +190,12 @@ def tile_selfattention3d_pb_kernel(
             nc.vector.quantize_mx(
                 out=codes[:].rearrange("p c n -> p (c n)").bitcast(FP8X4),
                 scales=scales[:].rearrange("p c n -> p (c n)"),
-                in_=grouped[:].rearrange("p c n -> p (c n)"),
+                in_=w_grouped[first_row_tile][:].rearrange("p c n -> p (c n)"),
             )
-            return codes, scales
+            weights[first_row_tile] = (codes, scales)
 
-        def product(out, t, member, weights, first, width):
-            w_codes, w_scales = weights
+        def product(out, t, member, first_row_tile, first, width):
+            w_codes, w_scales = weights[first_row_tile]
             for c in range(PASSES):
                 nc.tensor.matmul_mx(
                     out=out,
@@ -201,10 +211,8 @@ def tile_selfattention3d_pb_kernel(
         phi_banks = {}
         g_banks = {}
 
-        def products(t):
-            if t >= CHUNKS:
-                return
-            w_codes, w_scales = w_small
+        def theta_product(t):
+            w_codes, w_scales = weights[SMALL]
             theta_bank = psum.tile([P, MEMBERS * P], F32, tag="bank")
             for c in range(PASSES):
                 nc.tensor.matmul_mx(
@@ -217,24 +225,28 @@ def tile_selfattention3d_pb_kernel(
                     stop=(c == PASSES - 1),
                 )
             theta_banks[t] = theta_bank
+
+        def phi_product(t):
             phi_bank = psum.tile([P, MEMBERS, C_PHI], F32, tag="bank")
             for member in range(MEMBERS):
-                product(phi_bank[:, member, :], t, member, w_small, 0, C_PHI)
+                product(phi_bank[:, member, :], t, member, SMALL, 0, C_PHI)
             phi_banks[t] = phi_bank
+
+        def g_products(t):
             for member in range(MEMBERS):
                 g_bank = psum.tile([P, C_G], F32, tag="bank")
-                product(g_bank[:, 0:BLOCK], t, member, w_g_low, 0, BLOCK)
-                product(g_bank[:, BLOCK:C_G], t, member, w_g_high, 0, BLOCK)
+                product(g_bank[:, 0:BLOCK], t, member, G_LOW, 0, BLOCK)
+                product(g_bank[:, BLOCK:C_G], t, member, G_HIGH, 0, BLOCK)
                 g_banks[t, member] = g_bank
 
-        pooleds = {}
+        pooleds = [results.tile([P, C_G + C_PHI], F32, name="pooled") for t in range(CHUNKS)]
+        by_channels = {}
+        flipped_banks = {}
 
         def copy_first_member(t):
-            pooled = results.tile([P, C_G + C_PHI], F32, name="pooled")
-            nc.scalar.copy(out=pooled[:, 0:C_G], in_=g_banks[t, 0][:])
-            pooleds[t] = pooled
+            nc.scalar.copy(out=pooleds[t][:, 0:C_G], in_=g_banks[t, 0][:])
 
-        def tanh_theta_store(t):
+        def tanh_theta(t):
             by_channel = results.tile([P, CHUNK], F32, name="theta_by_channel")
             for di in range(2):
                 nc.scalar.activation(
@@ -248,11 +260,19 @@ def tile_selfattention3d_pb_kernel(
                     bias=bias_theta[:],
                     scale=1.0,
                 )
+            by_channels[t] = by_channel
+
+        def flip_theta(t):
             flipped = psum.tile([P, CHUNK // P, C_THETA], F32, tag="bank")
             for j in range(CHUNK // P):
-                nc.tensor.transpose(flipped[:, j, :], by_channel[:, j * P : (j + 1) * P], ident[:])
+                nc.tensor.transpose(
+                    flipped[:, j, :], by_channels[t][:, j * P : (j + 1) * P], ident[:]
+                )
+            flipped_banks[t] = flipped
+
+        def store_theta(t):
             theta = results.tile([P, CHUNK // P, C_THETA], F32, name="theta")
-            nc.scalar.copy(out=theta[:], in_=flipped[:])
+            nc.scalar.copy(out=theta[:], in_=flipped_banks[t][:])
             nc.sync.dma_start(out=theta_rows[t], in_=theta[:])
 
         def pool_phi(t):
@@ -271,39 +291,75 @@ def tile_selfattention3d_pb_kernel(
                 op=ALU.max,
             )
 
-        def add_pooled_bias_store(t):
+        def add_bias(engine, t, columns):
             pooled = pooleds[t]
-            adder = nc.vector if t == CHUNKS - 1 else nc.gpsimd
-            for columns in (slice(C_G, C_G + C_PHI), slice(0, C_G)):
-                adder.tensor_tensor(
-                    out=pooled[:, columns], in0=pooled[:, columns], in1=bias[:, columns], op=ALU.add
-                )
-            nc.sync.dma_start(out=g_rows[t], in_=pooled[:, 0:C_G])
+            engine.tensor_tensor(
+                out=pooled[:, columns], in0=pooled[:, columns], in1=bias[:, columns], op=ALU.add
+            )
+
+        g_columns = slice(0, C_G)
+        phi_columns = slice(C_G, C_G + C_PHI)
+
+        def store_g(t):
+            nc.sync.dma_start(out=g_rows[t], in_=pooleds[t][:, 0:C_G])
 
         def tanh_phi_store(t):
             phi = results.tile([P, C_PHI], F32, name="phi")
             nc.scalar.activation(out=phi[:], in_=pooleds[t][:, C_G:], func=ACT.Tanh)
             nc.sync.dma_start(out=phi_rows[t], in_=phi[:])
 
-        regroup(0)
-        regroup(1)
-        quantise(0, 0)
-        quantise(0, 1)
-        w_small = prepare_weights(4)
-        w_g_low = prepare_weights(0)
-        w_g_high = prepare_weights(2)
-        products(0)
-        for t in range(CHUNKS):
-            regroup(PASSES * t + 2)
-            regroup(PASSES * t + 3)
-            quantise(t + 1, 0)
-            quantise(t + 1, 1)
-            products(t + 1)
-            copy_first_member(t)
-            tanh_theta_store(t)
-            pool_phi(t)
-            max_g(t, 1)
-            max_g(t, 2)
-            max_g(t, 3)
-            add_pooled_bias_store(t)
-            tanh_phi_store(t)
+        with tc.manual_schedule():
+            nc.vector.memset(bias_rows[:], 0.0)
+            load_all()
+            constants()
+            regroup(0, 0)
+            spread_biases()
+            for block in (SMALL, G_LOW, G_HIGH):
+                transpose_weights(block)
+            copy_weights(SMALL)
+            regroup(0, 1)
+            quantise_weights(SMALL)
+            quantise(0, 0)
+            quantise(0, 1)
+            theta_product(0)
+            phi_product(0)
+            copy_weights(G_LOW)
+            quantise_weights(G_LOW)
+            copy_weights(G_HIGH)
+            regroup(1, 0)
+            quantise_weights(G_HIGH)
+            g_products(0)
+            tanh_theta(0)
+            pool_phi(0)
+            add_bias(nc.gpsimd, 0, phi_columns)
+            regroup(1, 1)
+            quantise(1, 0)
+            quantise(1, 1)
+            for t in range(CHUNKS):
+                ahead = t + 2 < CHUNKS
+                flip_theta(t)
+                if t + 1 < CHUNKS:
+                    theta_product(t + 1)
+                    phi_product(t + 1)
+                    g_products(t + 1)
+                if ahead:
+                    regroup(t + 2, 0)
+                copy_first_member(t)
+                if ahead:
+                    quantise(t + 2, 0)
+                max_g(t, 1)
+                if ahead:
+                    regroup(t + 2, 1)
+                max_g(t, 2)
+                if ahead:
+                    quantise(t + 2, 1)
+                max_g(t, 3)
+                store_theta(t)
+                tanh_phi_store(t)
+                last = t == CHUNKS - 1
+                add_bias(nc.vector if last else nc.gpsimd, t, g_columns)
+                store_g(t)
+                if not last:
+                    tanh_theta(t + 1)
+                    pool_phi(t + 1)
+                    add_bias(nc.vector if t + 1 == CHUNKS - 1 else nc.gpsimd, t + 1, phi_columns)

@@ -123,25 +123,22 @@ def tile_selfattention3d_pb_kernel(
             )
             nc.scalar.copy(out=bias_theta[:], in_=bias_theta_bank[:, 0:1])
 
-        def regroup_vector(t, c):
-            nc.vector.tensor_copy(
-                out=groupeds[t][:, c, 0:2, :, :].rearrange(
-                    "p dj (a b) k -> p a b k dj", a=WINDOW_ROWS
+        def regroup_rows(copy, t, c, di):
+            copy(
+                out=groupeds[t][:, c, 2 * di : 2 * (di + 1), :, :].rearrange(
+                    "p dj (a b2 b1) k -> p a b2 k b1 dj", a=WINDOW_ROWS, b1=2
                 ),
                 in_=raws[t][:, c, :, :].rearrange(
-                    "p k (a di b dj) -> p di a b k dj", a=WINDOW_ROWS, di=2, b=WINDOW_COLS, dj=2
-                )[:, 0],
+                    "p k (a di b2 b1 dj) -> p di a b2 k b1 dj",
+                    a=WINDOW_ROWS, di=2, b2=WINDOW_COLS // 2, b1=2, dj=2,
+                )[:, di],
             )
 
+        def regroup_vector(t, c):
+            regroup_rows(nc.vector.tensor_copy, t, c, 0)
+
         def regroup_scalar(t, c):
-            by_member = raws[t][:, c, :, :].rearrange(
-                "p k (a di b dj) -> p di dj a b k", a=WINDOW_ROWS, di=2, b=WINDOW_COLS, dj=2
-            )
-            for dj in range(2):
-                nc.scalar.copy(
-                    out=groupeds[t][:, c, 2 + dj, :, :].rearrange("p (a b) k -> p a b k", a=WINDOW_ROWS),
-                    in_=by_member[:, 1, dj],
-                )
+            regroup_rows(nc.scalar.copy, t, c, 1)
 
         def regroup(t, c):
             regroup_vector(t, c)

@@ -69,7 +69,7 @@ def tile_selfattention3d_pb_kernel(
         bias_rows = consts.tile([P, C_G + C_PHI + C_THETA], BF16)
         bias = consts.tile([P, C_G + C_PHI], F32)
         bias_theta = consts.tile([P, 1], F32)
-        ones = consts.tile([P, P], BF16)
+        ones = consts.tile([P, BANK], BF16)
         ident = consts.tile([P, P], F32)
         warm = consts.tile([P, 1], F32)
 
@@ -102,12 +102,19 @@ def tile_selfattention3d_pb_kernel(
             nc.scalar.activation(out=warm[:], in_=warm[:], func=ACT.Tanh)
             make_identity(nc, ident[:])
 
+        def start_warming():
+            return psum.tile([P, BANK], F32, tag="bank", name="warm_bank")
+
+        def keep_warm(bank, count):
+            for i in range(count):
+                nc.tensor.matmul(out=bank[:], lhsT=ones[:, 0:P], rhs=ones[:], start=True, stop=True)
+
         def spread_biases():
             for first, width in ((0, C_G), (C_G, C_PHI)):
                 bias_bank = psum.tile([P, BANK], F32, tag="bank")
                 nc.tensor.matmul(
                     out=bias_bank[:, 0:width],
-                    lhsT=ones[:],
+                    lhsT=ones[:, 0:P],
                     rhs=bias_rows[:, first : first + width],
                     start=True,
                     stop=True,
@@ -117,13 +124,16 @@ def tile_selfattention3d_pb_kernel(
             nc.tensor.matmul(
                 out=bias_theta_bank[:, 0:P],
                 lhsT=bias_rows[:, C_G + C_PHI :],
-                rhs=ones[:],
+                rhs=ones[:, 0:P],
                 start=True,
                 stop=True,
             )
             nc.scalar.copy(out=bias_theta[:], in_=bias_theta_bank[:, 0:1])
 
-        def regroup_rows(copy, t, c, di):
+        by_vector = nc.vector.tensor_copy
+        by_scalar = nc.scalar.copy
+
+        def regroup(t, c, di, copy):
             copy(
                 out=groupeds[t][:, c, 2 * di : 2 * (di + 1), :, :].rearrange(
                     "p dj (a b2 b1) k -> p a b2 k b1 dj", a=WINDOW_ROWS, b1=2
@@ -133,16 +143,6 @@ def tile_selfattention3d_pb_kernel(
                     a=WINDOW_ROWS, di=2, b2=WINDOW_COLS // 2, b1=2, dj=2,
                 )[:, di],
             )
-
-        def regroup_vector(t, c):
-            regroup_rows(nc.vector.tensor_copy, t, c, 0)
-
-        def regroup_scalar(t, c):
-            regroup_rows(nc.scalar.copy, t, c, 1)
-
-        def regroup(t, c):
-            regroup_vector(t, c)
-            regroup_scalar(t, c)
 
         def quantise(t, c):
             nc.vector.quantize_mx(
@@ -155,7 +155,7 @@ def tile_selfattention3d_pb_kernel(
         w_banks = {}
         weights = {}
 
-        def transpose_weights(first_row_tile):
+        def transpose_weights(first_row_tile, warm_bank):
             for c in range(PASSES):
                 w_bank = psum.tile([P, 2, HALVES, P], F32, tag="bank")
                 for r in range(2):
@@ -164,6 +164,7 @@ def tile_selfattention3d_pb_kernel(
                         pass_words = slice(HALVES * P * c + u, HALVES * P * (c + 1), HALVES)
                         nc.tensor.transpose(w_bank[:, r, u, :], words[:, pass_words], ident[:])
                 w_banks[first_row_tile, c] = w_bank
+                keep_warm(warm_bank, 1)
 
         def copy_weights(first_row_tile):
             grouped = consts.tile(
@@ -309,27 +310,33 @@ def tile_selfattention3d_pb_kernel(
             nc.vector.memset(bias_rows[:], 0.0)
             load_all()
             constants()
-            regroup(0, 0)
+            warm_bank = start_warming()
+            keep_warm(warm_bank, 8)
+            regroup(0, 0, 0, by_vector)
+            regroup(0, 0, 1, by_vector)
+            quantise(0, 0)
             spread_biases()
             for block in (SMALL, G_LOW, G_HIGH):
-                transpose_weights(block)
+                transpose_weights(block, warm_bank)
             copy_weights(SMALL)
-            regroup(0, 1)
+            regroup(0, 1, 0, by_vector)
+            regroup(0, 1, 1, by_vector)
             quantise_weights(SMALL)
-            quantise(0, 0)
             quantise(0, 1)
             theta_product(0)
             phi_product(0)
             copy_weights(G_LOW)
             quantise_weights(G_LOW)
             copy_weights(G_HIGH)
-            regroup(1, 0)
+            regroup(1, 0, 0, by_vector)
+            regroup(1, 0, 1, by_scalar)
             quantise_weights(G_HIGH)
             g_products(0)
             tanh_theta(0)
             pool_phi(0)
             add_bias(nc.gpsimd, 0, phi_columns)
-            regroup(1, 1)
+            regroup(1, 1, 0, by_vector)
+            regroup(1, 1, 1, by_scalar)
             quantise(1, 0)
             quantise(1, 1)
             for t in range(CHUNKS):
@@ -340,13 +347,15 @@ def tile_selfattention3d_pb_kernel(
                     phi_product(t + 1)
                     g_products(t + 1)
                 if ahead:
-                    regroup(t + 2, 0)
+                    regroup(t + 2, 0, 0, by_scalar if t + 3 == CHUNKS else by_vector)
+                    regroup(t + 2, 0, 1, by_scalar)
                 copy_first_member(t)
                 if ahead:
                     quantise(t + 2, 0)
                 max_g(t, 1)
                 if ahead:
-                    regroup(t + 2, 1)
+                    regroup(t + 2, 1, 0, by_vector)
+                    regroup(t + 2, 1, 1, by_scalar)
                 max_g(t, 2)
                 if ahead:
                     quantise(t + 2, 1)
@@ -359,4 +368,4 @@ def tile_selfattention3d_pb_kernel(
                 if not last:
                     tanh_theta(t + 1)
                     pool_phi(t + 1)
-                    add_bias(nc.vector if t + 1 == CHUNKS - 1 else nc.gpsimd, t + 1, phi_columns)
+                    add_bias(nc.gpsimd, t + 1, phi_columns)

@@ -281,11 +281,11 @@ def tile_selfattention3d_pb_kernel(
                 op=ALU.max,
             )
 
-        def max_g(t, member):
+        def max_g(t, member, columns):
             nc.vector.tensor_tensor(
-                out=pooleds[t][:, 0:C_G],
-                in0=g_banks[t, member][:],
-                in1=pooleds[t][:, 0:C_G],
+                out=pooleds[t][:, columns],
+                in0=g_banks[t, member][:, columns],
+                in1=pooleds[t][:, columns],
                 op=ALU.max,
             )
 
@@ -296,10 +296,11 @@ def tile_selfattention3d_pb_kernel(
             )
 
         g_columns = slice(0, C_G)
+        g_halves = (slice(0, BLOCK), slice(BLOCK, C_G))
         phi_columns = slice(C_G, C_G + C_PHI)
 
-        def store_g(t):
-            nc.sync.dma_start(out=g_rows[t], in_=pooleds[t][:, 0:C_G])
+        def store_g(t, columns):
+            nc.sync.dma_start(out=g_rows[t][:, columns], in_=pooleds[t][:, columns])
 
         def tanh_phi_store(t):
             phi = results.tile([P, C_PHI], F32, name="phi")
@@ -311,11 +312,12 @@ def tile_selfattention3d_pb_kernel(
             load_all()
             constants()
             warm_bank = start_warming()
-            keep_warm(warm_bank, 8)
+            keep_warm(warm_bank, 5)
             regroup(0, 0, 0, by_vector)
             regroup(0, 0, 1, by_vector)
             quantise(0, 0)
             spread_biases()
+            keep_warm(warm_bank, 2)
             for block in (SMALL, G_LOW, G_HIGH):
                 transpose_weights(block, warm_bank)
             copy_weights(SMALL)
@@ -332,40 +334,55 @@ def tile_selfattention3d_pb_kernel(
             regroup(1, 0, 1, by_scalar)
             quantise_weights(G_HIGH)
             g_products(0)
-            tanh_theta(0)
-            pool_phi(0)
-            add_bias(nc.gpsimd, 0, phi_columns)
             regroup(1, 1, 0, by_vector)
             regroup(1, 1, 1, by_scalar)
             quantise(1, 0)
+            pool_phi(0)
+            add_bias(nc.gpsimd, 0, phi_columns)
             quantise(1, 1)
             for t in range(CHUNKS):
-                ahead = t + 2 < CHUNKS
+                tanh_theta(t)
                 flip_theta(t)
                 if t + 1 < CHUNKS:
                     theta_product(t + 1)
                     phi_product(t + 1)
                     g_products(t + 1)
-                if ahead:
-                    regroup(t + 2, 0, 0, by_scalar if t + 3 == CHUNKS else by_vector)
-                    regroup(t + 2, 0, 1, by_scalar)
                 copy_first_member(t)
-                if ahead:
-                    quantise(t + 2, 0)
-                max_g(t, 1)
-                if ahead:
-                    regroup(t + 2, 1, 0, by_vector)
+                if t + 2 < CHUNKS:
+                    regroup(t + 2, 0, 0, by_vector)
+                    regroup(t + 2, 0, 1, by_scalar)
+                    max_g(t, 1, g_columns)
+                    regroup(t + 2, 1, 0, by_scalar if t + 3 == CHUNKS else by_vector)
                     regroup(t + 2, 1, 1, by_scalar)
-                max_g(t, 2)
-                if ahead:
+                    quantise(t + 2, 0)
+                    max_g(t, 2, g_columns)
                     quantise(t + 2, 1)
-                max_g(t, 3)
-                store_theta(t)
-                tanh_phi_store(t)
-                last = t == CHUNKS - 1
-                add_bias(nc.vector if last else nc.gpsimd, t, g_columns)
-                store_g(t)
-                if not last:
-                    tanh_theta(t + 1)
+                    max_g(t, 3, g_columns)
+                    add_bias(nc.gpsimd, t, g_columns)
+                    store_g(t, g_columns)
+                    store_theta(t)
+                    tanh_phi_store(t)
+                    if t == 0:
+                        pool_phi(1)
+                        add_bias(nc.gpsimd, 1, phi_columns)
+                elif t + 2 == CHUNKS:
+                    max_g(t, 1, g_columns)
+                    pool_phi(t)
+                    add_bias(nc.gpsimd, t, phi_columns)
+                    max_g(t, 2, g_columns)
                     pool_phi(t + 1)
                     add_bias(nc.gpsimd, t + 1, phi_columns)
+                    max_g(t, 3, g_columns)
+                    add_bias(nc.gpsimd, t, g_columns)
+                    store_g(t, g_columns)
+                    store_theta(t)
+                    tanh_phi_store(t)
+                else:
+                    for member in range(1, MEMBERS):
+                        for columns in g_halves:
+                            max_g(t, member, columns)
+                    store_theta(t)
+                    tanh_phi_store(t)
+                    for columns in g_halves:
+                        add_bias(nc.vector, t, columns)
+                        store_g(t, columns)

@@ -136,12 +136,19 @@ def tile_selfattention3d_pb_kernel(
         def regroup(t, c, di, copy):
             copy(
                 out=groupeds[t][:, c, 2 * di : 2 * (di + 1), :, :].rearrange(
-                    "p dj (a b2 b1) k -> p a b2 k b1 dj", a=WINDOW_ROWS, b1=2
+                    "p dj (a b2 b1) k -> p a b2 k b1 dj", a=WINDOW_ROWS, b1=4
                 ),
                 in_=raws[t][:, c, :, :].rearrange(
                     "p k (a di b2 b1 dj) -> p di a b2 k b1 dj",
-                    a=WINDOW_ROWS, di=2, b2=WINDOW_COLS // 2, b1=2, dj=2,
+                    a=WINDOW_ROWS, di=2, b2=WINDOW_COLS // 4, b1=4, dj=2,
                 )[:, di],
+            )
+
+        def quantise_both(t):
+            nc.vector.quantize_mx(
+                out=x_codes[t][:].rearrange("p c m w -> p (c m w)").bitcast(FP8X4),
+                scales=x_scales[t][:].rearrange("p c m w -> p (c m w)"),
+                in_=groupeds[t][:].rearrange("p c m w k -> p (c m w k)"),
             )
 
         def quantise(t, c):
@@ -337,52 +344,45 @@ def tile_selfattention3d_pb_kernel(
             regroup(1, 1, 0, by_vector)
             regroup(1, 1, 1, by_scalar)
             quantise(1, 0)
-            pool_phi(0)
-            add_bias(nc.gpsimd, 0, phi_columns)
             quantise(1, 1)
             for t in range(CHUNKS):
+                last = t == CHUNKS - 1
                 tanh_theta(t)
-                flip_theta(t)
-                if t + 1 < CHUNKS:
+                if not last:
                     theta_product(t + 1)
                     phi_product(t + 1)
                     g_products(t + 1)
+                flip_theta(t)
                 copy_first_member(t)
                 if t + 2 < CHUNKS:
+                    helper = by_scalar if t + 3 == CHUNKS else by_vector
+                    pool_phi(t)
+                    add_bias(nc.gpsimd, t, phi_columns)
                     regroup(t + 2, 0, 0, by_vector)
                     regroup(t + 2, 0, 1, by_scalar)
                     max_g(t, 1, g_columns)
-                    regroup(t + 2, 1, 0, by_scalar if t + 3 == CHUNKS else by_vector)
+                    regroup(t + 2, 1, 0, helper)
                     regroup(t + 2, 1, 1, by_scalar)
                     quantise(t + 2, 0)
                     max_g(t, 2, g_columns)
                     quantise(t + 2, 1)
-                    max_g(t, 3, g_columns)
-                    add_bias(nc.gpsimd, t, g_columns)
-                    store_g(t, g_columns)
-                    store_theta(t)
-                    tanh_phi_store(t)
-                    if t == 0:
-                        pool_phi(1)
-                        add_bias(nc.gpsimd, 1, phi_columns)
-                elif t + 2 == CHUNKS:
+                else:
                     max_g(t, 1, g_columns)
                     pool_phi(t)
                     add_bias(nc.gpsimd, t, phi_columns)
-                    max_g(t, 2, g_columns)
-                    pool_phi(t + 1)
-                    add_bias(nc.gpsimd, t + 1, phi_columns)
+                    for columns in g_halves if last else (g_columns,):
+                        max_g(t, 2, columns)
+                if t > 0:
+                    store_theta(t - 1)
+                    tanh_phi_store(t - 1)
+                if last:
+                    store_theta(t)
+                    tanh_phi_store(t)
+                    for engine, columns in zip((nc.gpsimd, nc.vector), g_halves):
+                        max_g(t, 3, columns)
+                        add_bias(engine, t, columns)
+                        store_g(t, columns)
+                else:
                     max_g(t, 3, g_columns)
                     add_bias(nc.gpsimd, t, g_columns)
                     store_g(t, g_columns)
-                    store_theta(t)
-                    tanh_phi_store(t)
-                else:
-                    for member in range(1, MEMBERS):
-                        for columns in g_halves:
-                            max_g(t, member, columns)
-                    store_theta(t)
-                    tanh_phi_store(t)
-                    for columns in g_halves:
-                        add_bias(nc.vector, t, columns)
-                        store_g(t, columns)

from contextlib import ExitStack

import concourse.mybir as mybir
from concourse.masks import make_identity

FLOPS = 2 * (128 + 128 + 512) * 1024 * 2048

BF16 = mybir.dt.bfloat16
F32 = mybir.dt.float32
U32 = mybir.dt.uint32
U8 = mybir.dt.uint8
FP8X4 = mybir.dt.float8_e4m3fn_x4
ALU = mybir.AluOpType
ACT = mybir.ActivationFunctionType

P = 128
PACK = 4
PASSES = 2
HALVES = 2
CHANNELS = 1024
CHUNKS = 4
CHUNK = 512
WINDOW_ROWS = 16
WINDOW_COLS = 8
MEMBERS = 4
C_G = 512
C_PHI = 128
C_THETA = 128
BLOCK = 256
BANK = 512
PSUM_BANKS = 8
SMALL = 4
G_LOW = 0
G_HIGH = 2


def tile_selfattention3d_pb_kernel(
    tc, x, w_theta, b_theta, w_phi, b_phi, w_g, b_g, out_0, out_1, out_2
):
    nc = tc.nc

    x_pieces = x.rearrange("o (c p k) f i j -> (o c) p k (f i j)", c=PASSES, p=P, k=PACK)
    theta_rows = out_0.rearrange("o (t j p) c -> (o t) p j c", t=CHUNKS, p=P)
    phi_rows = out_1.rearrange("o (t w) c -> (o t) w c", t=CHUNKS)
    g_rows = out_2.rearrange("o (t w) c -> (o t) w c", t=CHUNKS)
    w_g_tiles = w_g.rearrange("(r p) k -> p r k", p=P)

    with ExitStack() as ctx:
        consts = ctx.enter_context(tc.tile_pool(name="consts", bufs=1))
        per_chunk = ctx.enter_context(tc.tile_pool(name="per_chunk", bufs=CHUNKS))
        results = ctx.enter_context(tc.tile_pool(name="results", bufs=CHUNKS))
        psum = ctx.enter_context(tc.psum_pool(name="psum", bufs=PSUM_BANKS))

        raws = [per_chunk.tile([P, PASSES, PACK, CHUNK], BF16, name="raw") for t in range(CHUNKS)]
        groupeds = [
            per_chunk.tile([P, PASSES, MEMBERS, P, PACK], BF16, align_bytes=64, name="grouped")
            for t in range(CHUNKS)
        ]
        x_codes = [
            per_chunk.tile([P, PASSES, MEMBERS, P], U32, align_bytes=64, name="x_codes")
            for t in range(CHUNKS)
        ]
        x_scales = [
            per_chunk.tile([P, PASSES, MEMBERS, P], U8, align_bytes=64, name="x_scales")
            for t in range(CHUNKS)
        ]

        w_rows = consts.tile([P, 6, CHANNELS], BF16)
        bias_rows = consts.tile([P, C_G + C_PHI + C_THETA], BF16)
        bias = consts.tile([P, C_G + C_PHI], F32)
        bias_theta = consts.tile([P, 1], F32)
        ones = consts.tile([P, BANK], BF16)
        ident = consts.tile([P, P], F32)
        warm = consts.tile([P, 1], F32)

        def load_x(t, c):
            nc.sync.dma_start(
                out=raws[t][:, c, :, :], in_=x_pieces[c, :, :, t * CHUNK : (t + 1) * CHUNK]
            )

        def load_all():
            load_x(0, 0)
            for vec, first, width in (
                (b_g, 0, C_G), (b_phi, C_G, C_PHI), (b_theta, C_G + C_PHI, C_THETA)
            ):
                nc.sync.dma_start(
                    out=bias_rows[0:1, first : first + width],
                    in_=vec.rearrange("(o n) -> o n", o=1),
                )
            nc.sync.dma_start(out=w_rows[:, 4, :], in_=w_phi)
            nc.sync.dma_start(out=w_rows[:, 5, :], in_=w_theta)
            load_x(0, 1)
            nc.sync.dma_start(out=w_rows[:, 0:2, :], in_=w_g_tiles[:, 0:2, :])
            nc.sync.dma_start(out=w_rows[:, 2:4, :], in_=w_g_tiles[:, 2:4, :])
            for t in range(1, CHUNKS):
                for c in range(PASSES):
                    load_x(t, c)

        def constants():
            nc.vector.memset(warm[:], 0.0)
            nc.vector.memset(ones[:], 1.0)
            nc.scalar.activation(out=warm[:], in_=warm[:], func=ACT.Tanh)
            make_identity(nc, ident[:])

        def start_warming():
            return psum.tile([P, BANK], F32, tag="bank", name="warm_bank")

        def keep_warm(bank, count):
            for i in range(count):
                nc.tensor.matmul(out=bank[:], lhsT=ones[:, 0:P], rhs=ones[:], start=True, stop=True)

        def spread_biases():
            for first, width in ((0, C_G), (C_G, C_PHI)):
                bias_bank = psum.tile([P, BANK], F32, tag="bank")
                nc.tensor.matmul(
                    out=bias_bank[:, 0:width],
                    lhsT=ones[:, 0:P],
                    rhs=bias_rows[:, first : first + width],
                    start=True,
                    stop=True,
                )
                nc.scalar.copy(out=bias[:, first : first + width], in_=bias_bank[:, 0:width])
            bias_theta_bank = psum.tile([P, BANK], F32, tag="bank")
            nc.tensor.matmul(
                out=bias_theta_bank[:, 0:P],
                lhsT=bias_rows[:, C_G + C_PHI :],
                rhs=ones[:, 0:P],
                start=True,
                stop=True,
            )
            nc.scalar.copy(out=bias_theta[:], in_=bias_theta_bank[:, 0:1])

        by_vector = nc.vector.tensor_copy
        by_scalar = nc.scalar.copy

        def regroup(t, c, di, copy):
            copy(
                out=groupeds[t][:, c, 2 * di : 2 * (di + 1), :, :].rearrange(
                    "p dj (a b2 b1) k -> p a b2 k b1 dj", a=WINDOW_ROWS, b1=4
                ),
                in_=raws[t][:, c, :, :].rearrange(
                    "p k (a di b2 b1 dj) -> p di a b2 k b1 dj",
                    a=WINDOW_ROWS, di=2, b2=WINDOW_COLS // 4, b1=4, dj=2,
                )[:, di],
            )

        def quantise_both(t):
            nc.vector.quantize_mx(
                out=x_codes[t][:].rearrange("p c m w -> p (c m w)").bitcast(FP8X4),
                scales=x_scales[t][:].rearrange("p c m w -> p (c m w)"),
                in_=groupeds[t][:].rearrange("p c m w k -> p (c m w k)"),
            )

        def quantise(t, c):
            nc.vector.quantize_mx(
                out=x_codes[t][:, c, :, :].rearrange("p m w -> p (m w)").bitcast(FP8X4),
                scales=x_scales[t][:, c, :, :].rearrange("p m w -> p (m w)"),
                in_=groupeds[t][:, c, :, :, :].rearrange("p m w k -> p (m w k)"),
            )

        w_grouped = {}
        w_banks = {}
        weights = {}

        def transpose_weights(first_row_tile, warm_bank):
            for c in range(PASSES):
                w_bank = psum.tile([P, 2, HALVES, P], F32, tag="bank")
                for r in range(2):
                    words = w_rows[:, first_row_tile + r, :].bitcast(F32)
                    for u in range(HALVES):
                        pass_words = slice(HALVES * P * c + u, HALVES * P * (c + 1), HALVES)
                        nc.tensor.transpose(w_bank[:, r, u, :], words[:, pass_words], ident[:])
                w_banks[first_row_tile, c] = w_bank
                keep_warm(warm_bank, 1)

        def copy_weights(first_row_tile):
            grouped = consts.tile(
                [P, PASSES, BLOCK * PACK], BF16, align_bytes=64,
                name="w_grouped%d" % first_row_tile,
            )
            for c in range(PASSES):
                nc.scalar.copy(
                    out=grouped[:, c, :].bitcast(F32).rearrange("p (r o u) -> p r o u", r=2, u=HALVES),
                    in_=w_banks[first_row_tile, c][:].rearrange("p r u o -> p r o u"),
                )
            w_grouped[first_row_tile] = grouped

        def quantise_weights(first_row_tile):
            codes = consts.tile(
                [P, PASSES, BLOCK], U32, align_bytes=64, name="w_codes%d" % first_row_tile
            )
            scales = consts.tile(
                [P, PASSES, BLOCK], U8, align_bytes=64, name="w_scales%d" % first_row_tile
            )
            nc.vector.quantize_mx(
                out=codes[:].rearrange("p c n -> p (c n)").bitcast(FP8X4),
                scales=scales[:].rearrange("p c n -> p (c n)"),
                in_=w_grouped[first_row_tile][:].rearrange("p c n -> p (c n)"),
            )
            weights[first_row_tile] = (codes, scales)

        def product(out, t, member, first_row_tile, first, width):
            w_codes, w_scales = weights[first_row_tile]
            for c in range(PASSES):
                nc.tensor.matmul_mx(
                    out=out,
                    lhsT=x_codes[t][:, c, member, :].bitcast(FP8X4),
                    lhsT_scale=x_scales[t][:, c, member, :],
                    rhs=w_codes[:, c, first : first + width].bitcast(FP8X4),
                    rhs_scale=w_scales[:, c, first : first + width],
                    start=(c == 0),
                    stop=(c == PASSES - 1),
                )

        theta_banks = {}
        phi_banks = {}
        g_banks = {}

        def theta_product(t):
            w_codes, w_scales = weights[SMALL]
            theta_bank = psum.tile([P, MEMBERS * P], F32, tag="bank")
            for c in range(PASSES):
                nc.tensor.matmul_mx(
                    out=theta_bank[:],
                    lhsT=w_codes[:, c, C_PHI : C_PHI + C_THETA].bitcast(FP8X4),
                    lhsT_scale=w_scales[:, c, C_PHI : C_PHI + C_THETA],
                    rhs=x_codes[t][:, c, :, :].rearrange("p m w -> p (m w)").bitcast(FP8X4),
                    rhs_scale=x_scales[t][:, c, :, :].rearrange("p m w -> p (m w)"),
                    start=(c == 0),
                    stop=(c == PASSES - 1),
                )
            theta_banks[t] = theta_bank

        def phi_product(t):
            phi_bank = psum.tile([P, MEMBERS, C_PHI], F32, tag="bank")
            for member in range(MEMBERS):
                product(phi_bank[:, member, :], t, member, SMALL, 0, C_PHI)
            phi_banks[t] = phi_bank

        def g_products(t):
            for member in range(MEMBERS):
                g_bank = psum.tile([P, C_G], F32, tag="bank")
                product(g_bank[:, 0:BLOCK], t, member, G_LOW, 0, BLOCK)
                product(g_bank[:, BLOCK:C_G], t, member, G_HIGH, 0, BLOCK)
                g_banks[t, member] = g_bank

        pooleds = [results.tile([P, C_G + C_PHI], F32, name="pooled") for t in range(CHUNKS)]
        by_channels = {}
        flipped_banks = {}

        def copy_first_member(t):
            nc.scalar.copy(out=pooleds[t][:, 0:C_G], in_=g_banks[t, 0][:])

        def tanh_theta(t):
            by_channel = results.tile([P, CHUNK], F32, name="theta_by_channel")
            for di in range(2):
                nc.scalar.activation(
                    out=by_channel[:].rearrange(
                        "p (a di b dj) -> p di a b dj", a=WINDOW_ROWS, di=2, b=WINDOW_COLS, dj=2
                    )[:, di],
                    in_=theta_banks[t][:].rearrange(
                        "p (di dj a b) -> p di a b dj", di=2, dj=2, a=WINDOW_ROWS, b=WINDOW_COLS
                    )[:, di],
                    func=ACT.Tanh,
                    bias=bias_theta[:],
                    scale=1.0,
                )
            by_channels[t] = by_channel

        def flip_theta(t):
            flipped = psum.tile([P, CHUNK // P, C_THETA], F32, tag="bank")
            for j in range(CHUNK // P):
                nc.tensor.transpose(
                    flipped[:, j, :], by_channels[t][:, j * P : (j + 1) * P], ident[:]
                )
            flipped_banks[t] = flipped

        def store_theta(t):
            theta = results.tile([P, CHUNK // P, C_THETA], F32, name="theta")
            nc.scalar.copy(out=theta[:], in_=flipped_banks[t][:])
            nc.sync.dma_start(out=theta_rows[t], in_=theta[:])

        def pool_phi(t):
            nc.vector.tensor_reduce(
                out=pooleds[t][:, C_G:],
                in_=phi_banks[t][:].rearrange("p m c -> p c m"),
                axis=mybir.AxisListType.X,
                op=ALU.max,
            )

        def max_g(t, member, columns):
            nc.vector.tensor_tensor(
                out=pooleds[t][:, columns],
                in0=g_banks[t, member][:, columns],
                in1=pooleds[t][:, columns],
                op=ALU.max,
            )

        def add_bias(engine, t, columns):
            pooled = pooleds[t]
            engine.tensor_tensor(
                out=pooled[:, columns], in0=pooled[:, columns], in1=bias[:, columns], op=ALU.add
            )

        g_columns = slice(0, C_G)
        g_halves = (slice(0, BLOCK), slice(BLOCK, C_G))
        phi_columns = slice(C_G, C_G + C_PHI)

        def store_g(t, columns):
            nc.sync.dma_start(out=g_rows[t][:, columns], in_=pooleds[t][:, columns])

        def tanh_phi_store(t):
            phi = results.tile([P, C_PHI], F32, name="phi")
            nc.scalar.activation(out=phi[:], in_=pooleds[t][:, C_G:], func=ACT.Tanh)
            nc.sync.dma_start(out=phi_rows[t], in_=phi[:])

        with tc.manual_schedule():
            nc.vector.memset(bias_rows[:], 0.0)
            load_all()
            constants()
            warm_bank = start_warming()
            keep_warm(warm_bank, 5)
            regroup(0, 0, 0, by_vector)
            regroup(0, 0, 1, by_vector)
            quantise(0, 0)
            spread_biases()
            keep_warm(warm_bank, 2)
            for block in (SMALL, G_LOW, G_HIGH):
                transpose_weights(block, warm_bank)
            copy_weights(SMALL)
            regroup(0, 1, 0, by_vector)
            regroup(0, 1, 1, by_vector)
            quantise_weights(SMALL)
            quantise(0, 1)
            theta_product(0)
            phi_product(0)
            copy_weights(G_LOW)
            quantise_weights(G_LOW)
            copy_weights(G_HIGH)
            regroup(1, 0, 0, by_vector)
            regroup(1, 0, 1, by_scalar)
            quantise_weights(G_HIGH)
            g_products(0)
            regroup(1, 1, 0, by_vector)
            regroup(1, 1, 1, by_scalar)
            quantise(1, 0)
            quantise(1, 1)
            for t in range(CHUNKS):
                last = t == CHUNKS - 1
                tanh_theta(t)
                if not last:
                    theta_product(t + 1)
                    phi_product(t + 1)
                    g_products(t + 1)
                flip_theta(t)
                copy_first_member(t)
                if t + 2 < CHUNKS:
                    helper = by_scalar if t + 3 == CHUNKS else by_vector
                    pool_phi(t)
                    add_bias(nc.gpsimd, t, phi_columns)
                    regroup(t + 2, 0, 0, by_vector)
                    regroup(t + 2, 0, 1, by_scalar)
                    max_g(t, 1, g_columns)
                    regroup(t + 2, 1, 0, helper)
                    regroup(t + 2, 1, 1, by_scalar)
                    quantise(t + 2, 0)
                    max_g(t, 2, g_columns)
                    quantise(t + 2, 1)
                else:
                    max_g(t, 1, g_columns)
                    pool_phi(t)
                    add_bias(nc.gpsimd, t, phi_columns)
                    for columns in g_halves if last else (g_columns,):
                        max_g(t, 2, columns)
                if t > 0:
                    store_theta(t - 1)
                    tanh_phi_store(t - 1)
                if last:
                    store_theta(t)
                    tanh_phi_store(t)
                    for engine, columns in zip((nc.gpsimd, nc.vector), g_halves):
                        max_g(t, 3, columns)
                        add_bias(engine, t, columns)
                        store_g(t, columns)
                else:
                    max_g(t, 3, g_columns)
                    add_bias(nc.gpsimd, t, g_columns)
                    store_g(t, g_columns)
